import numpy as np
import ml_dtypes


def mxq(x, axis, fmt="e4m3"):
    dtype, down = {"e4m3": (ml_dtypes.float8_e4m3fn, 7), "e5m2": (ml_dtypes.float8_e5m2, 14)}[fmt]
    v = np.moveaxis(np.asarray(x, np.float32).astype(ml_dtypes.bfloat16).astype(np.float64), axis, -1)
    blocks = v.reshape(v.shape[:-1] + (-1, 32))
    amax = np.abs(blocks).max(-1, keepdims=True)
    byte = np.maximum(np.where(amax > 0, np.frexp(amax)[1] - 1 + 127, 0) - down, 1)
    scale = np.exp2(byte - 127.0)
    codes = (blocks / scale).astype(np.float32).astype(dtype).astype(np.float64)
    return np.moveaxis((codes * scale).reshape(v.shape), -1, axis)


WIDE = False


def mx_kscale(k):
    if not WIDE:
        return np.ones(k)
    levels = np.array([10, -10, 5, -5, 0])
    a = np.random.permutation(np.resize(levels, k // 512 * 4)).reshape(k // 512, 4)
    idx = np.arange(k)
    return np.exp2(a[idx // 512, idx % 128 // 32])


BF16 = ml_dtypes.bfloat16


def bf(x):
    return np.asarray(x, np.float32).astype(BF16)


def f64(x):
    return np.asarray(x).astype(np.float64)


N, C, H, W, CO, KS, ST = 16, 64, 35, 35, 128, 4, 1
KK = KS * KS
F = C * KK
RUN = np.lcm(KK, 32)


def im2col(x, k, s):
    n, c, h, w = x.shape
    ho = (h - k) // s + 1
    wo = (w - k) // s + 1
    cols = np.stack([x[:, :, i:i + s * (ho - 1) + 1:s, j:j + s * (wo - 1) + 1:s] for i in range(k) for j in range(k)], axis=2)
    cols = cols.transpose(1, 2, 0, 3, 4).reshape(c * k * k, n * ho * wo)
    return cols, (n, ho, wo)


def setup_inputs():
    sc = np.repeat(mx_kscale(F)[::RUN], RUN // KK)
    sf = np.repeat(sc, KK)
    return {"x": bf(np.random.standard_normal((N, C, H, W)) * sc[None, :, None, None]),
            "weight": bf(np.random.uniform(0.0, 1.0, (CO, F)) * 1.7 / np.sqrt(F) / sf[None, :]),
            "bias": bf(np.random.uniform(-1.0, 1.0, (CO, 1)) * 0.5)}


def reference(x, weight, bias):
    cols, (n, ho, wo) = im2col(f64(x), KS, ST)
    flat = (mxq(f64(weight), 1, "e4m3") @ mxq(cols, 0, "e4m3")) + f64(bias)
    return flat.reshape(weight.shape[0], n, ho, wo).transpose(1, 0, 2, 3)

@@ -1,0 +1,132 @@
+from contextlib import ExitStack
+
+import concourse.mybir as mybir
+from concourse.masks import make_identity
+
+BF16 = mybir.dt.bfloat16
+F32 = mybir.dt.float32
+U32 = mybir.dt.uint32
+U8 = mybir.dt.uint8
+FP8X4 = mybir.dt.float8_e4m3fn_x4
+IDENT = mybir.ActivationFunctionType.Identity
+
+FLOPS = 2 * 128 * 1024 * 16384
+
+P = 128
+PAIRS = 8
+IMG = 35 * 35
+PITCH = 1280
+ROW = 128
+
+
+def tile_sparseconv2d_t_kernel(tc, x, weight, bias, out):
+    nc = tc.nc
+    with ExitStack() as ctx:
+        const = ctx.enter_context(tc.tile_pool(name="const", bufs=1))
+        spool = ctx.enter_context(tc.tile_pool(name="win", bufs=3))
+        qpool = ctx.enter_context(tc.tile_pool(name="codes", bufs=4))
+        opool = ctx.enter_context(tc.tile_pool(name="res", bufs=4))
+        psum = ctx.enter_context(tc.psum_pool(name="acc", bufs=8))
+
+        xr = x.rearrange("n c h w -> (n c) (h w)").rearrange("(m k r) f -> r k m f", m=PAIRS, k=16, r=8)
+        xs = const.tile([P, PAIRS, PITCH], BF16)
+
+        def load_x(m0, m1):
+            for r in range(8):
+                p0 = (r // 2) * 32 + (r % 2)
+                nc.sync.dma_start(out=xs[p0:p0 + 31:2, m0:m1, 0:IMG], in_=xr[r][:, m0:m1, :])
+
+        w_sb = const.tile([P, 1024], BF16)
+        nc.gpsimd.dma_start(out=w_sb[:], in_=weight)
+        load_x(0, 1)
+        b16 = const.tile([P, 1], BF16)
+        with nc.allow_non_contiguous_dma(reason="one bias value a partition"):
+            nc.gpsimd.dma_start(out=b16[:], in_=bias)
+        load_x(1, 2)
+        load_x(2, 4)
+        load_x(4, 8)
+
+        ident = const.tile([P, P], F32)
+        make_identity(nc, ident[:])
+        bf = const.tile([P, 1], F32)
+        nc.vector.tensor_copy(out=bf[:], in_=b16[:])
+
+        wp = const.tile([P, 2048], F32)
+        nc.vector.memset(wp[:], 0.0)
+        w_words = w_sb[:].bitcast(F32).rearrange("o (k a e t) -> o t a k e", k=8, a=4, e=2, t=8)
+        for nh in range(2):
+            dst = wp[:, nh * 1024:(nh + 1) * 1024].rearrange(
+                "o (t a h k e) -> o t a h k e", t=8, a=4, h=2, k=8, e=2)[:, :, :, nh, :, :]
+            nc.vector.tensor_copy(out=dst, in_=w_words)
+        grouped = const.tile([P, 4096], BF16, align_bytes=64)
+        gw = grouped[:].bitcast(F32)
+        for bank in range(4):
+            pw = psum.tile([P, 512], F32, tag="acc", name="pw%d" % bank)
+            for j in range(4):
+                beta = bank * 4 + j
+                nc.tensor.transpose(pw[:, j * P:(j + 1) * P], wp[:, beta * P:(beta + 1) * P], ident[:])
+            dst = gw[:, bank * 512:(bank + 1) * 512].rearrange("p (s o u) -> p s o u", s=2, o=P, u=2)
+            src = pw[:].rearrange("p (s u o) -> p s o u", s=2, u=2, o=P)
+            if bank % 2 == 0:
+                nc.vector.tensor_copy(out=dst, in_=src)
+            else:
+                nc.scalar.copy(out=dst, in_=src)
+        wq = const.tile([P, 1024], U32, align_bytes=64)
+        wsc = const.tile([P, 1024], U8, align_bytes=64)
+        nc.vector.quantize_mx(out=wq[:].bitcast(FP8X4), scales=wsc[:], in_=grouped[:])
+
+        def compact(m):
+            win = spool.tile([P, 36 * ROW], BF16, align_bytes=64, tag="win", name="win%d" % m)
+            sv = win[:].rearrange("p (h t s e) -> p h t s e", h=18, t=2, s=4, e=32)
+            sw = win[:].bitcast(F32).rearrange("p (h t s e) -> p h t s e", h=18, t=2, s=4, e=16)
+            xe = xs[:, m, 0:1260].rearrange("p (h e) -> p h e", e=70)
+            xw = xs[:, m, 0:1260].bitcast(F32).rearrange("p (h e) -> p h e", e=35)
+            for hp in range(2):
+                rows = 18 - hp
+                for rho in range(4):
+                    start = 35 * hp + rho
+                    even = start % 2 == 0
+                    if m == 0:
+                        on_vector = (not even) or (hp == 1 and rho == 3)
+                    else:
+                        on_vector = (not even) and hp == 0
+                    if on_vector:
+                        nc.vector.tensor_copy(out=sv[:, 0:rows, hp, rho, :], in_=xe[:, 0:rows, start:start + 32])
+                    elif even:
+                        nc.scalar.copy(out=sw[:, 0:rows, hp, rho, :],
+                                       in_=xw[:, 0:rows, start // 2:start // 2 + 16])
+                    else:
+                        nc.scalar.copy(out=sv[:, 0:rows, hp, rho, :], in_=xe[:, 0:rows, start:start + 32])
+            return win
+
+        nxt = compact(0)
+        for m in range(PAIRS):
+            win = nxt
+            accs = [psum.tile([P, 512], F32, tag="acc", name="acc%d_%d" % (m, b)) for b in range(4)]
+            for i in range(4):
+                cd = qpool.tile([P, 1024], U32, align_bytes=64, tag="cd", name="cd%d_%d" % (m, i))
+                sc = qpool.tile([P, 1024], U8, align_bytes=64, tag="sc", name="sc%d_%d" % (m, i))
+                nc.vector.quantize_mx(out=cd[:].bitcast(FP8X4), scales=sc[:],
+                                      in_=win[:, i * ROW:i * ROW + 4096])
+                for hf in range(2):
+                    for nh in range(2):
+                        s = nh * 4 + i
+                        nc.tensor.matmul_mx(
+                            out=accs[nh * 2 + hf][:],
+                            lhsT=wq[:, s * P:(s + 1) * P].bitcast(FP8X4),
+                            lhsT_scale=wsc[:, s * P:(s + 1) * P],
+                            rhs=cd[:, hf * 512:(hf + 1) * 512].bitcast(FP8X4),
+                            rhs_scale=sc[:, hf * 512:(hf + 1) * 512],
+                            start=(i == 0),
+                            stop=(i == 3),
+                        )
+                if i == 0 and m + 1 < PAIRS:
+                    nxt = compact(m + 1)
+            for nh in range(2):
+                ob = opool.tile([P, 1024], F32, tag="ob", name="ob%d_%d" % (m, nh))
+                for hf in range(2):
+                    nc.scalar.activation(
+                        out=ob[:, hf * 512:(hf + 1) * 512].rearrange("o (r q s) -> o r q s", r=16, q=8, s=4),
+                        in_=accs[nh * 2 + hf][:].rearrange("o (r s q) -> o r q s", r=16, s=4, q=8),
+                        func=IDENT, bias=bf[:, 0:1], scale=1.0)
+                nc.sync.dma_start(out=out[2 * m + nh].rearrange("o p q -> o (p q)"), in_=ob[:])

@@ -9,6 +9,7 @@ U32 = mybir.dt.uint32
 U8 = mybir.dt.uint8
 FP8X4 = mybir.dt.float8_e4m3fn_x4
 IDENT = mybir.ActivationFunctionType.Identity
+ADD = mybir.AluOpType.add
 
 FLOPS = 2 * 128 * 1024 * 16384
 
@@ -17,39 +18,75 @@ PAIRS = 8
 IMG = 35 * 35
 PITCH = 1280
 ROW = 128
+VEC_SHARE = ((0, 1), (0, 3))
 
 
 def tile_sparseconv2d_t_kernel(tc, x, weight, bias, out):
     nc = tc.nc
     with ExitStack() as ctx:
         const = ctx.enter_context(tc.tile_pool(name="const", bufs=1))
-        spool = ctx.enter_context(tc.tile_pool(name="win", bufs=3))
-        qpool = ctx.enter_context(tc.tile_pool(name="codes", bufs=4))
+        spool = ctx.enter_context(tc.tile_pool(name="win", bufs=4))
+        qpool = ctx.enter_context(tc.tile_pool(name="codes", bufs=6))
         opool = ctx.enter_context(tc.tile_pool(name="res", bufs=4))
         psum = ctx.enter_context(tc.psum_pool(name="acc", bufs=8))
+        ctx.enter_context(tc.manual_schedule())
 
         xr = x.rearrange("n c h w -> (n c) (h w)").rearrange("(m k r) f -> r k m f", m=PAIRS, k=16, r=8)
-        xs = const.tile([P, PAIRS, PITCH], BF16)
+        groups = ((0, 1), (1, 2), (2, 4), (4, 8))
+        xs = {}
+        for m0, m1 in groups:
+            xg = const.tile([P, m1 - m0, PITCH], BF16, name="xs%d" % m0)
+            for m in range(m0, m1):
+                xs[m] = xg[:, m - m0, :]
+            xs[(m0, m1)] = xg
 
-        def load_x(m0, m1):
-            for r in range(8):
-                p0 = (r // 2) * 32 + (r % 2)
-                nc.sync.dma_start(out=xs[p0:p0 + 31:2, m0:m1, 0:IMG], in_=xr[r][:, m0:m1, :])
+        def load_x(queue, r, m0, m1):
+            p0 = (r // 2) * 32 + (r % 2)
+            queue.dma_start(out=xs[(m0, m1)][p0:p0 + 31:2, :, 0:IMG], in_=xr[r][:, m0:m1, :])
 
         w_sb = const.tile([P, 1024], BF16)
         nc.gpsimd.dma_start(out=w_sb[:], in_=weight)
-        load_x(0, 1)
+        for r in range(8):
+            load_x(nc.sync, r, 0, 1)
         b16 = const.tile([P, 1], BF16)
         with nc.allow_non_contiguous_dma(reason="one bias value a partition"):
             nc.gpsimd.dma_start(out=b16[:], in_=bias)
-        load_x(1, 2)
-        load_x(2, 4)
-        load_x(4, 8)
+        for m0, m1 in groups[1:]:
+            for r in range(8):
+                load_x(nc.sync, r, m0, m1)
 
         ident = const.tile([P, P], F32)
         make_identity(nc, ident[:])
+        warm = const.tile([P, 2], F32)
+        nc.vector.memset(warm[:], 0.0)
+        nc.scalar.activation(out=warm[:, 1:2], in_=warm[:, 0:1], func=IDENT)
         bf = const.tile([P, 1], F32)
-        nc.vector.tensor_copy(out=bf[:], in_=b16[:])
+        nc.gpsimd.tensor_copy(out=bf[:], in_=b16[:])
+
+        wins = {}
+
+        def copies(m, engine_is_vector, share):
+            if m not in wins:
+                wins[m] = spool.tile([P, 36 * ROW], BF16, align_bytes=64, tag="win", name="win%d" % m)
+            win = wins[m]
+            sv = win[:].rearrange("p (h t s e) -> p h t s e", h=18, t=2, s=4, e=32)
+            sw = win[:].bitcast(F32).rearrange("p (h t s e) -> p h t s e", h=18, t=2, s=4, e=16)
+            xe = xs[m][:, 0:1260].rearrange("p (h e) -> p h e", e=70)
+            xw = xs[m][:, 0:1260].bitcast(F32).rearrange("p (h e) -> p h e", e=35)
+            for hp, rho in share:
+                rows = 18 - hp
+                start = 35 * hp + rho
+                if engine_is_vector:
+                    nc.vector.tensor_copy(out=sv[:, 0:rows, hp, rho, :], in_=xe[:, 0:rows, start:start + 32])
+                elif start % 2 == 0:
+                    nc.scalar.copy(out=sw[:, 0:rows, hp, rho, :], in_=xw[:, 0:rows, start // 2:start // 2 + 16])
+                else:
+                    nc.scalar.copy(out=sv[:, 0:rows, hp, rho, :], in_=xe[:, 0:rows, start:start + 32])
+
+        every = tuple((hp, rho) for hp in range(2) for rho in range(4))
+        aligned = tuple(c for c in every if (35 * c[0] + c[1]) % 2 == 0)
+        odd = tuple(c for c in every if c not in aligned)
+        sca_share = tuple(c for c in every if c not in VEC_SHARE)
 
         wp = const.tile([P, 2048], F32)
         nc.vector.memset(wp[:], 0.0)
@@ -58,6 +95,8 @@ def tile_sparseconv2d_t_kernel(tc, x, weight, bias, out):
             dst = wp[:, nh * 1024:(nh + 1) * 1024].rearrange(
                 "o (t a h k e) -> o t a h k e", t=8, a=4, h=2, k=8, e=2)[:, :, :, nh, :, :]
             nc.vector.tensor_copy(out=dst, in_=w_words)
+        copies(0, True, odd)
+        copies(0, False, aligned)
         grouped = const.tile([P, 4096], BF16, align_bytes=64)
         gw = grouped[:].bitcast(F32)
         for bank in range(4):
@@ -65,68 +104,88 @@ def tile_sparseconv2d_t_kernel(tc, x, weight, bias, out):
             for j in range(4):
                 beta = bank * 4 + j
                 nc.tensor.transpose(pw[:, j * P:(j + 1) * P], wp[:, beta * P:(beta + 1) * P], ident[:])
-            dst = gw[:, bank * 512:(bank + 1) * 512].rearrange("p (s o u) -> p s o u", s=2, o=P, u=2)
-            src = pw[:].rearrange("p (s u o) -> p s o u", s=2, u=2, o=P)
-            if bank % 2 == 0:
-                nc.vector.tensor_copy(out=dst, in_=src)
-            else:
-                nc.scalar.copy(out=dst, in_=src)
+            nc.scalar.copy(out=gw[:, bank * 512:(bank + 1) * 512].rearrange("p (s o u) -> p s o u", s=2, o=P, u=2),
+                           in_=pw[:].rearrange("p (s u o) -> p s o u", s=2, u=2, o=P))
         wq = const.tile([P, 1024], U32, align_bytes=64)
         wsc = const.tile([P, 1024], U8, align_bytes=64)
-        nc.vector.quantize_mx(out=wq[:].bitcast(FP8X4), scales=wsc[:], in_=grouped[:])
 
-        def compact(m):
-            win = spool.tile([P, 36 * ROW], BF16, align_bytes=64, tag="win", name="win%d" % m)
-            sv = win[:].rearrange("p (h t s e) -> p h t s e", h=18, t=2, s=4, e=32)
-            sw = win[:].bitcast(F32).rearrange("p (h t s e) -> p h t s e", h=18, t=2, s=4, e=16)
-            xe = xs[:, m, 0:1260].rearrange("p (h e) -> p h e", e=70)
-            xw = xs[:, m, 0:1260].bitcast(F32).rearrange("p (h e) -> p h e", e=35)
-            for hp in range(2):
-                rows = 18 - hp
-                for rho in range(4):
-                    start = 35 * hp + rho
-                    even = start % 2 == 0
-                    if m == 0:
-                        on_vector = (not even) or (hp == 1 and rho == 3)
-                    else:
-                        on_vector = (not even) and hp == 0
-                    if on_vector:
-                        nc.vector.tensor_copy(out=sv[:, 0:rows, hp, rho, :], in_=xe[:, 0:rows, start:start + 32])
-                    elif even:
-                        nc.scalar.copy(out=sw[:, 0:rows, hp, rho, :],
-                                       in_=xw[:, 0:rows, start // 2:start // 2 + 16])
-                    else:
-                        nc.scalar.copy(out=sv[:, 0:rows, hp, rho, :], in_=xe[:, 0:rows, start:start + 32])
-            return win
+        accs = {}
 
-        nxt = compact(0)
-        for m in range(PAIRS):
-            win = nxt
-            accs = [psum.tile([P, 512], F32, tag="acc", name="acc%d_%d" % (m, b)) for b in range(4)]
-            for i in range(4):
-                cd = qpool.tile([P, 1024], U32, align_bytes=64, tag="cd", name="cd%d_%d" % (m, i))
-                sc = qpool.tile([P, 1024], U8, align_bytes=64, tag="sc", name="sc%d_%d" % (m, i))
-                nc.vector.quantize_mx(out=cd[:].bitcast(FP8X4), scales=sc[:],
-                                      in_=win[:, i * ROW:i * ROW + 4096])
-                for hf in range(2):
-                    for nh in range(2):
-                        s = nh * 4 + i
-                        nc.tensor.matmul_mx(
-                            out=accs[nh * 2 + hf][:],
-                            lhsT=wq[:, s * P:(s + 1) * P].bitcast(FP8X4),
-                            lhsT_scale=wsc[:, s * P:(s + 1) * P],
-                            rhs=cd[:, hf * 512:(hf + 1) * 512].bitcast(FP8X4),
-                            rhs_scale=sc[:, hf * 512:(hf + 1) * 512],
-                            start=(i == 0),
-                            stop=(i == 3),
-                        )
-                if i == 0 and m + 1 < PAIRS:
-                    nxt = compact(m + 1)
+        def quantise(m, i, hf, halves):
+            width = 512 * halves
+            cd = qpool.tile([P, width], U32, align_bytes=64, tag="cd%d" % halves, name="cd%d_%d_%d" % (m, i, hf))
+            sc = qpool.tile([P, width], U8, align_bytes=64, tag="sc%d" % halves, name="sc%d_%d_%d" % (m, i, hf))
+            first = (hf * 16 + i) * ROW
+            nc.vector.quantize_mx(out=cd[:].bitcast(FP8X4), scales=sc[:], in_=wins[m][:, first:first + 4 * width])
+            return cd, sc
+
+        def multiply(m, i, hf, halves, cd, sc):
+            for h in range(halves):
+                for nh in range(2):
+                    key = (m, nh, hf + h)
+                    if key not in accs:
+                        accs[key] = psum.tile([P, 512], F32, tag="acc", name="acc%d_%d_%d" % key)
+                    s = nh * 4 + i
+                    nc.tensor.matmul_mx(
+                        out=accs[key][:],
+                        lhsT=wq[:, s * P:(s + 1) * P].bitcast(FP8X4),
+                        lhsT_scale=wsc[:, s * P:(s + 1) * P],
+                        rhs=cd[:, h * 512:(h + 1) * 512].bitcast(FP8X4),
+                        rhs_scale=sc[:, h * 512:(h + 1) * 512],
+                        start=(i == 0),
+                        stop=(i == 3),
+                    )
+
+        def leave(dst, m, nh, hf, on_vector):
+            src = accs[(m, nh, hf)][:].rearrange("o (r s q) -> o r q s", r=16, s=4, q=8)
+            dst = dst.rearrange("o (r q s) -> o r q s", r=16, q=8, s=4)
+            if on_vector:
+                nc.vector.tensor_scalar(out=dst, in0=src, scalar1=bf[:, 0:1], scalar2=None, op0=ADD)
+            else:
+                nc.scalar.activation(out=dst, in_=src, func=IDENT, bias=bf[:, 0:1], scale=1.0)
+
+        def finish(m):
             for nh in range(2):
                 ob = opool.tile([P, 1024], F32, tag="ob", name="ob%d_%d" % (m, nh))
                 for hf in range(2):
-                    nc.scalar.activation(
-                        out=ob[:, hf * 512:(hf + 1) * 512].rearrange("o (r q s) -> o r q s", r=16, q=8, s=4),
-                        in_=accs[nh * 2 + hf][:].rearrange("o (r s q) -> o r q s", r=16, s=4, q=8),
-                        func=IDENT, bias=bf[:, 0:1], scale=1.0)
+                    leave(ob[:, hf * 512:(hf + 1) * 512], m, nh, hf, False)
                 nc.sync.dma_start(out=out[2 * m + nh].rearrange("o p q -> o (p q)"), in_=ob[:])
+
+        def finish_half(m, hf, vector_helps):
+            for nh in range(2):
+                ob = opool.tile([P, 512], F32, tag="obh", name="obh%d_%d_%d" % (m, nh, hf))
+                leave(ob[:], m, nh, hf, vector_helps and nh == 0)
+                nc.sync.dma_start(out=out[2 * m + nh].rearrange("o p q -> o (p q)")[:, hf * 512:(hf + 1) * 512],
+                                  in_=ob[:])
+
+        copies(1, False, sca_share)
+        q0 = quantise(0, 0, 0, 2)
+        q1 = quantise(0, 1, 0, 2)
+        nc.vector.quantize_mx(out=wq[:].bitcast(FP8X4), scales=wsc[:], in_=grouped[:])
+        multiply(0, 0, 0, 2, q0[0], q0[1])
+        multiply(0, 1, 0, 2, q1[0], q1[1])
+        copies(1, True, VEC_SHARE[0:1])
+        q2 = quantise(0, 2, 0, 2)
+        multiply(0, 2, 0, 2, q2[0], q2[1])
+        copies(1, True, VEC_SHARE[1:2])
+        q3 = quantise(0, 3, 0, 2)
+        multiply(0, 3, 0, 2, q3[0], q3[1])
+        copies(2, False, sca_share)
+
+        for m in range(1, PAIRS - 1):
+            finish(m - 1)
+            if m + 2 < PAIRS:
+                copies(m + 2, False, sca_share)
+            for i in range(4):
+                cd, sc = quantise(m, i, 0, 2)
+                multiply(m, i, 0, 2, cd, sc)
+                if i < 2:
+                    copies(m + 1, True, VEC_SHARE[i:i + 1])
+
+        m = PAIRS - 1
+        finish(m - 1)
+        for hf in range(2):
+            for i in range(4):
+                cd, sc = quantise(m, i, hf, 1)
+                multiply(m, i, hf, 1, cd, sc)
+            finish_half(m, hf, hf == 1)

@@ -18,7 +18,7 @@ PAIRS = 8
 IMG = 35 * 35
 PITCH = 1280
 ROW = 128
-VEC_SHARE = ((0, 1), (0, 3))
+VEC_SHARE = ((0, 1),)
 
 
 def tile_sparseconv2d_t_kernel(tc, x, weight, bias, out):
@@ -45,8 +45,9 @@ def tile_sparseconv2d_t_kernel(tc, x, weight, bias, out):
             queue.dma_start(out=xs[(m0, m1)][p0:p0 + 31:2, :, 0:IMG], in_=xr[r][:, m0:m1, :])
 
         w_sb = const.tile([P, 1024], BF16)
-        nc.gpsimd.dma_start(out=w_sb[:], in_=weight)
-        for r in range(8):
+        nc.sync.dma_start(out=w_sb[:], in_=weight)
+        load_x(nc.gpsimd, 7, 0, 1)
+        for r in range(7):
             load_x(nc.sync, r, 0, 1)
         b16 = const.tile([P, 1], BF16)
         with nc.allow_non_contiguous_dma(reason="one bias value a partition"):
@@ -91,10 +92,11 @@ def tile_sparseconv2d_t_kernel(tc, x, weight, bias, out):
         wp = const.tile([P, 2048], F32)
         nc.vector.memset(wp[:], 0.0)
         w_words = w_sb[:].bitcast(F32).rearrange("o (k a e t) -> o t a k e", k=8, a=4, e=2, t=8)
-        for nh in range(2):
-            dst = wp[:, nh * 1024:(nh + 1) * 1024].rearrange(
-                "o (t a h k e) -> o t a h k e", t=8, a=4, h=2, k=8, e=2)[:, :, :, nh, :, :]
-            nc.vector.tensor_copy(out=dst, in_=w_words)
+        for quarter in range(4):
+            i2, nh = quarter // 2, quarter % 2
+            dst = wp[:, quarter * 512:(quarter + 1) * 512].rearrange(
+                "o (t a h k e) -> o t a h k e", t=4, a=4, h=2, k=8, e=2)[:, :, :, nh, :, :]
+            nc.vector.tensor_copy(out=dst, in_=w_words[:, i2 * 4:(i2 + 1) * 4, :, :, :])
         copies(0, True, odd)
         copies(0, False, aligned)
         grouped = const.tile([P, 4096], BF16, align_bytes=64)
@@ -119,13 +121,45 @@ def tile_sparseconv2d_t_kernel(tc, x, weight, bias, out):
             nc.vector.quantize_mx(out=cd[:].bitcast(FP8X4), scales=sc[:], in_=wins[m][:, first:first + 4 * width])
             return cd, sc
 
+        def quarter_step(m, i, qt):
+            cd = qpool.tile([P, 256], U32, align_bytes=64, tag="cdq", name="cdq%d_%d_%d" % (m, i, qt))
+            sc = qpool.tile([P, 256], U8, align_bytes=64, tag="scq", name="scq%d_%d_%d" % (m, i, qt))
+            first = (qt * 8 + i) * ROW
+            nc.vector.quantize_mx(out=cd[:].bitcast(FP8X4), scales=sc[:], in_=wins[m][:, first:first + 1024])
+            for nh in range(2):
+                key = (m, nh, "q%d" % qt)
+                if key not in accs:
+                    accs[key] = psum.tile([P, 256], F32, tag="acc", name="accq%d_%d_%d" % (m, nh, qt))
+                s = (i // 2) * 4 + nh * 2 + i % 2
+                nc.tensor.matmul_mx(
+                    out=accs[key][:],
+                    lhsT=wq[:, s * P:(s + 1) * P].bitcast(FP8X4),
+                    lhsT_scale=wsc[:, s * P:(s + 1) * P],
+                    rhs=cd[:].bitcast(FP8X4),
+                    rhs_scale=sc[:],
+                    start=(i == 0),
+                    stop=(i == 3),
+                )
+
+        def finish_quarter(m, qt, vector_helps):
+            for nh in range(2):
+                ob = opool.tile([P, 256], F32, tag="obq", name="obq%d_%d_%d" % (m, nh, qt))
+                src = accs[(m, nh, "q%d" % qt)][:].rearrange("o (r s q) -> o r q s", r=8, s=4, q=8)
+                dst = ob[:].rearrange("o (r q s) -> o r q s", r=8, q=8, s=4)
+                if vector_helps and nh == 0:
+                    nc.vector.tensor_scalar(out=dst, in0=src, scalar1=bf[:, 0:1], scalar2=None, op0=ADD)
+                else:
+                    nc.scalar.activation(out=dst, in_=src, func=IDENT, bias=bf[:, 0:1], scale=1.0)
+                nc.sync.dma_start(out=out[2 * m + nh].rearrange("o p q -> o (p q)")[:, qt * 256:(qt + 1) * 256],
+                                  in_=ob[:])
+
         def multiply(m, i, hf, halves, cd, sc):
             for h in range(halves):
                 for nh in range(2):
                     key = (m, nh, hf + h)
                     if key not in accs:
                         accs[key] = psum.tile([P, 512], F32, tag="acc", name="acc%d_%d_%d" % key)
-                    s = nh * 4 + i
+                    s = (i // 2) * 4 + nh * 2 + i % 2
                     nc.tensor.matmul_mx(
                         out=accs[key][:],
                         lhsT=wq[:, s * P:(s + 1) * P].bitcast(FP8X4),
@@ -160,10 +194,11 @@ def tile_sparseconv2d_t_kernel(tc, x, weight, bias, out):
 
         copies(1, False, sca_share)
         q0 = quantise(0, 0, 0, 2)
-        q1 = quantise(0, 1, 0, 2)
-        nc.vector.quantize_mx(out=wq[:].bitcast(FP8X4), scales=wsc[:], in_=grouped[:])
+        nc.vector.quantize_mx(out=wq[:, 0:512].bitcast(FP8X4), scales=wsc[:, 0:512], in_=grouped[:, 0:2048])
         multiply(0, 0, 0, 2, q0[0], q0[1])
+        q1 = quantise(0, 1, 0, 2)
         multiply(0, 1, 0, 2, q1[0], q1[1])
+        nc.vector.quantize_mx(out=wq[:, 512:1024].bitcast(FP8X4), scales=wsc[:, 512:1024], in_=grouped[:, 2048:4096])
         copies(1, True, VEC_SHARE[0:1])
         q2 = quantise(0, 2, 0, 2)
         multiply(0, 2, 0, 2, q2[0], q2[1])
@@ -184,8 +219,11 @@ def tile_sparseconv2d_t_kernel(tc, x, weight, bias, out):
 
         m = PAIRS - 1
         finish(m - 1)
-        for hf in range(2):
+        for i in range(4):
+            cd, sc = quantise(m, i, 0, 1)
+            multiply(m, i, 0, 1, cd, sc)
+        finish_half(m, 0, False)
+        for qt in (2, 3):
             for i in range(4):
-                cd, sc = quantise(m, i, hf, 1)
-                multiply(m, i, hf, 1, cd, sc)
-            finish_half(m, hf, hf == 1)
+                quarter_step(m, i, qt)
+            finish_quarter(m, qt, qt == 3)

@@ -18,7 +18,7 @@ PAIRS = 8
 IMG = 35 * 35
 PITCH = 1280
 ROW = 128
-VEC_SHARE = ((0, 1),)
+VEC_SHARE = ()
 
 
 def tile_sparseconv2d_t_kernel(tc, x, weight, bias, out):

@@ -18,7 +18,6 @@ PAIRS = 8
 IMG = 35 * 35
 PITCH = 1280
 ROW = 128
-VEC_SHARE = ()
 
 
 def tile_sparseconv2d_t_kernel(tc, x, weight, bias, out):
@@ -47,17 +46,22 @@ def tile_sparseconv2d_t_kernel(tc, x, weight, bias, out):
         w_sb = const.tile([P, 1024], BF16)
         nc.sync.dma_start(out=w_sb[:], in_=weight)
         load_x(nc.gpsimd, 7, 0, 1)
-        for r in range(7):
+        for r in (0, 1, 2, 3):
+            load_x(nc.scalar, r, 0, 1)
+        for r in (4, 5, 6):
             load_x(nc.sync, r, 0, 1)
-        b16 = const.tile([P, 1], BF16)
-        with nc.allow_non_contiguous_dma(reason="one bias value a partition"):
-            nc.gpsimd.dma_start(out=b16[:], in_=bias)
         for m0, m1 in groups[1:]:
             for r in range(8):
                 load_x(nc.sync, r, m0, m1)
 
+        wp = const.tile([P, 8 * 144], F32)
+        runs = wp[:].rearrange("o (t g k) -> o t g k", t=8, g=9, k=16)
+        nc.gpsimd.memset(runs[:, :, 0:9:2, :], 0.0)
         ident = const.tile([P, P], F32)
         make_identity(nc, ident[:])
+        b16 = const.tile([P, 1], BF16)
+        with nc.allow_non_contiguous_dma(reason="one bias value a partition"):
+            nc.gpsimd.dma_start(out=b16[:], in_=bias)
         warm = const.tile([P, 2], F32)
         nc.vector.memset(warm[:], 0.0)
         nc.scalar.activation(out=warm[:, 1:2], in_=warm[:, 0:1], func=IDENT)
@@ -66,48 +70,53 @@ def tile_sparseconv2d_t_kernel(tc, x, weight, bias, out):
 
         wins = {}
 
-        def copies(m, engine_is_vector, share):
+        def window_tile(m):
             if m not in wins:
                 wins[m] = spool.tile([P, 36 * ROW], BF16, align_bytes=64, tag="win", name="win%d" % m)
-            win = wins[m]
-            sv = win[:].rearrange("p (h t s e) -> p h t s e", h=18, t=2, s=4, e=32)
-            sw = win[:].bitcast(F32).rearrange("p (h t s e) -> p h t s e", h=18, t=2, s=4, e=16)
-            xe = xs[m][:, 0:1260].rearrange("p (h e) -> p h e", e=70)
-            xw = xs[m][:, 0:1260].bitcast(F32).rearrange("p (h e) -> p h e", e=35)
-            for hp, rho in share:
-                rows = 18 - hp
-                start = 35 * hp + rho
-                if engine_is_vector:
-                    nc.vector.tensor_copy(out=sv[:, 0:rows, hp, rho, :], in_=xe[:, 0:rows, start:start + 32])
-                elif start % 2 == 0:
-                    nc.scalar.copy(out=sw[:, 0:rows, hp, rho, :], in_=xw[:, 0:rows, start // 2:start // 2 + 16])
-                else:
-                    nc.scalar.copy(out=sv[:, 0:rows, hp, rho, :], in_=xe[:, 0:rows, start:start + 32])
+            return wins[m]
 
-        every = tuple((hp, rho) for hp in range(2) for rho in range(4))
+        def copies(m, on_vector, on_scalar):
+            win = window_tile(m)
+            to = win[:].rearrange("p (h t s e) -> p h t s e", h=18, t=2, s=4, e=32)
+            to_words = win[:].bitcast(F32).rearrange("p (h t s e) -> p h t s e", h=18, t=2, s=4, e=16)
+            rows_of = xs[m][:, 0:1260].rearrange("p (h e) -> p h e", e=70)
+            words_of = xs[m][:, 0:1260].bitcast(F32).rearrange("p (h e) -> p h e", e=35)
+            for parity, s in on_vector + on_scalar:
+                n = 18 - parity
+                start = 35 * parity + s
+                if (parity, s) in on_vector:
+                    nc.vector.tensor_copy(out=to[:, 0:n, parity, s, :], in_=rows_of[:, 0:n, start:start + 32])
+                elif start % 2 == 0:
+                    nc.scalar.copy(out=to_words[:, 0:n, parity, s, :], in_=words_of[:, 0:n, start // 2:start // 2 + 16])
+                else:
+                    nc.scalar.copy(out=to[:, 0:n, parity, s, :], in_=rows_of[:, 0:n, start:start + 32])
+
+        every = tuple((parity, s) for parity in range(2) for s in range(4))
         aligned = tuple(c for c in every if (35 * c[0] + c[1]) % 2 == 0)
         odd = tuple(c for c in every if c not in aligned)
-        sca_share = tuple(c for c in every if c not in VEC_SHARE)
 
-        wp = const.tile([P, 2048], F32)
-        nc.vector.memset(wp[:], 0.0)
         w_words = w_sb[:].bitcast(F32).rearrange("o (k a e t) -> o t a k e", k=8, a=4, e=2, t=8)
-        for quarter in range(4):
-            i2, nh = quarter // 2, quarter % 2
-            dst = wp[:, quarter * 512:(quarter + 1) * 512].rearrange(
-                "o (t a h k e) -> o t a h k e", t=4, a=4, h=2, k=8, e=2)[:, :, :, nh, :, :]
-            nc.vector.tensor_copy(out=dst, in_=w_words[:, i2 * 4:(i2 + 1) * 4, :, :, :])
-        copies(0, True, odd)
-        copies(0, False, aligned)
+
+        def sort_weights(i2):
+            dst = wp[:].rearrange("o (t g k e) -> o t g k e", t=8, g=9, k=8, e=2)[:, i2 * 4:i2 * 4 + 4, 1:9:2, :, :]
+            nc.vector.tensor_copy(out=dst, in_=w_words[:, i2 * 4:i2 * 4 + 4, :, :, :])
+
         grouped = const.tile([P, 4096], BF16, align_bytes=64)
         gw = grouped[:].bitcast(F32)
-        for bank in range(4):
+        pws = {}
+
+        def transpose_weights(bank):
+            i2, nh = bank // 2, bank % 2
             pw = psum.tile([P, 512], F32, tag="acc", name="pw%d" % bank)
+            pws[bank] = pw
             for j in range(4):
-                beta = bank * 4 + j
-                nc.tensor.transpose(pw[:, j * P:(j + 1) * P], wp[:, beta * P:(beta + 1) * P], ident[:])
+                first = (i2 * 4 + j) * 144 + 16 * (1 - nh)
+                nc.tensor.transpose(pw[:, j * P:(j + 1) * P], wp[:, first:first + P], ident[:])
+
+        def regroup_weights(bank):
             nc.scalar.copy(out=gw[:, bank * 512:(bank + 1) * 512].rearrange("p (s o u) -> p s o u", s=2, o=P, u=2),
-                           in_=pw[:].rearrange("p (s u o) -> p s o u", s=2, u=2, o=P))
+                           in_=pws[bank][:].rearrange("p (s u o) -> p s o u", s=2, u=2, o=P))
+
         wq = const.tile([P, 1024], U32, align_bytes=64)
         wsc = const.tile([P, 1024], U8, align_bytes=64)
 
@@ -153,9 +162,9 @@ def tile_sparseconv2d_t_kernel(tc, x, weight, bias, out):
                 nc.sync.dma_start(out=out[2 * m + nh].rearrange("o p q -> o (p q)")[:, qt * 256:(qt + 1) * 256],
                                   in_=ob[:])
 
-        def multiply(m, i, hf, halves, cd, sc):
+        def multiply(m, i, hf, halves, cd, sc, images=(0, 1)):
             for h in range(halves):
-                for nh in range(2):
+                for nh in images:
                     key = (m, nh, hf + h)
                     if key not in accs:
                         accs[key] = psum.tile([P, 512], F32, tag="acc", name="acc%d_%d_%d" % key)
@@ -192,30 +201,43 @@ def tile_sparseconv2d_t_kernel(tc, x, weight, bias, out):
                 nc.sync.dma_start(out=out[2 * m + nh].rearrange("o p q -> o (p q)")[:, hf * 512:(hf + 1) * 512],
                                   in_=ob[:])
 
-        copies(1, False, sca_share)
-        q0 = quantise(0, 0, 0, 2)
-        nc.vector.quantize_mx(out=wq[:, 0:512].bitcast(FP8X4), scales=wsc[:, 0:512], in_=grouped[:, 0:2048])
-        multiply(0, 0, 0, 2, q0[0], q0[1])
-        q1 = quantise(0, 1, 0, 2)
-        multiply(0, 1, 0, 2, q1[0], q1[1])
-        nc.vector.quantize_mx(out=wq[:, 512:1024].bitcast(FP8X4), scales=wsc[:, 512:1024], in_=grouped[:, 2048:4096])
-        copies(1, True, VEC_SHARE[0:1])
-        q2 = quantise(0, 2, 0, 2)
-        multiply(0, 2, 0, 2, q2[0], q2[1])
-        copies(1, True, VEC_SHARE[1:2])
-        q3 = quantise(0, 3, 0, 2)
-        multiply(0, 3, 0, 2, q3[0], q3[1])
-        copies(2, False, sca_share)
+        def quantise_weights(b0, b1):
+            nc.vector.quantize_mx(out=wq[:, b0 * 256:b1 * 256].bitcast(FP8X4), scales=wsc[:, b0 * 256:b1 * 256],
+                                  in_=grouped[:, b0 * 1024:b1 * 1024])
+
+        codes = {}
+        sort_weights(0)
+        sort_weights(1)
+        copies(0, odd, ())
+        copies(0, (), aligned)
+        transpose_weights(0)
+        transpose_weights(1)
+        transpose_weights(2)
+        transpose_weights(3)
+        regroup_weights(0)
+        regroup_weights(1)
+        regroup_weights(2)
+        regroup_weights(3)
+        copies(1, (), every)
+        codes[(0, 0)] = quantise(0, 0, 0, 2)
+        quantise_weights(0, 2)
+        multiply(0, 0, 0, 2, *codes[(0, 0)])
+        codes[(1, 0)] = quantise(0, 1, 0, 2)
+        multiply(0, 1, 0, 2, *codes[(1, 0)])
+        quantise_weights(2, 4)
+        codes[(2, 0)] = quantise(0, 2, 0, 2)
+        multiply(0, 2, 0, 2, *codes[(2, 0)])
+        codes[(3, 0)] = quantise(0, 3, 0, 2)
+        multiply(0, 3, 0, 2, *codes[(3, 0)])
+        copies(2, (), every)
 
         for m in range(1, PAIRS - 1):
             finish(m - 1)
             if m + 2 < PAIRS:
-                copies(m + 2, False, sca_share)
+                copies(m + 2, (), every)
             for i in range(4):
                 cd, sc = quantise(m, i, 0, 2)
                 multiply(m, i, 0, 2, cd, sc)
-                if i < 2:
-                    copies(m + 1, True, VEC_SHARE[i:i + 1])
 
         m = PAIRS - 1
         finish(m - 1)

@@ -56,7 +56,7 @@ def tile_sparseconv2d_t_kernel(tc, x, weight, bias, out):
 
         wp = const.tile([P, 8 * 144], F32)
         runs = wp[:].rearrange("o (t g k) -> o t g k", t=8, g=9, k=16)
-        nc.gpsimd.memset(runs[:, :, 0:9:2, :], 0.0)
+        nc.vector.memset(runs[:, :, 0:9:2, :], 0.0)
         ident = const.tile([P, P], F32)
         make_identity(nc, ident[:])
         b16 = const.tile([P, 1], BF16)

@@ -50,7 +50,12 @@ def tile_sparseconv2d_t_kernel(tc, x, weight, bias, out):
             load_x(nc.scalar, r, 0, 1)
         for r in (4, 5, 6):
             load_x(nc.sync, r, 0, 1)
-        for m0, m1 in groups[1:]:
+        for r in range(8):
+            load_x(nc.sync, r, 1, 2)
+        b16 = const.tile([P, 1], BF16)
+        with nc.allow_non_contiguous_dma(reason="one bias value a partition"):
+            nc.sync.dma_start(out=b16[:], in_=bias)
+        for m0, m1 in groups[2:]:
             for r in range(8):
                 load_x(nc.sync, r, m0, m1)
 
@@ -59,14 +64,9 @@ def tile_sparseconv2d_t_kernel(tc, x, weight, bias, out):
         nc.vector.memset(runs[:, :, 0:9:2, :], 0.0)
         ident = const.tile([P, P], F32)
         make_identity(nc, ident[:])
-        b16 = const.tile([P, 1], BF16)
-        with nc.allow_non_contiguous_dma(reason="one bias value a partition"):
-            nc.gpsimd.dma_start(out=b16[:], in_=bias)
         warm = const.tile([P, 2], F32)
         nc.vector.memset(warm[:], 0.0)
         nc.scalar.activation(out=warm[:, 1:2], in_=warm[:, 0:1], func=IDENT)
-        bf = const.tile([P, 1], F32)
-        nc.gpsimd.tensor_copy(out=bf[:], in_=b16[:])
 
         wins = {}
 
@@ -156,9 +156,9 @@ def tile_sparseconv2d_t_kernel(tc, x, weight, bias, out):
                 src = accs[(m, nh, "q%d" % qt)][:].rearrange("o (r s q) -> o r q s", r=8, s=4, q=8)
                 dst = ob[:].rearrange("o (r q s) -> o r q s", r=8, q=8, s=4)
                 if vector_helps and nh == 0:
-                    nc.vector.tensor_scalar(out=dst, in0=src, scalar1=bf[:, 0:1], scalar2=None, op0=ADD)
+                    nc.vector.tensor_scalar(out=dst, in0=src, scalar1=b16[:, 0:1], scalar2=None, op0=ADD)
                 else:
-                    nc.scalar.activation(out=dst, in_=src, func=IDENT, bias=bf[:, 0:1], scale=1.0)
+                    nc.scalar.activation(out=dst, in_=src, func=IDENT, bias=b16[:, 0:1], scale=1.0)
                 nc.sync.dma_start(out=out[2 * m + nh].rearrange("o p q -> o (p q)")[:, qt * 256:(qt + 1) * 256],
                                   in_=ob[:])
 
@@ -183,9 +183,9 @@ def tile_sparseconv2d_t_kernel(tc, x, weight, bias, out):
             src = accs[(m, nh, hf)][:].rearrange("o (r s q) -> o r q s", r=16, s=4, q=8)
             dst = dst.rearrange("o (r q s) -> o r q s", r=16, q=8, s=4)
             if on_vector:
-                nc.vector.tensor_scalar(out=dst, in0=src, scalar1=bf[:, 0:1], scalar2=None, op0=ADD)
+                nc.vector.tensor_scalar(out=dst, in0=src, scalar1=b16[:, 0:1], scalar2=None, op0=ADD)
             else:
-                nc.scalar.activation(out=dst, in_=src, func=IDENT, bias=bf[:, 0:1], scale=1.0)
+                nc.scalar.activation(out=dst, in_=src, func=IDENT, bias=b16[:, 0:1], scale=1.0)
 
         def finish(m):
             for nh in range(2):

from contextlib import ExitStack

import concourse.mybir as mybir
from concourse.masks import make_identity

BF16 = mybir.dt.bfloat16
F32 = mybir.dt.float32
U32 = mybir.dt.uint32
U8 = mybir.dt.uint8
FP8X4 = mybir.dt.float8_e4m3fn_x4
IDENT = mybir.ActivationFunctionType.Identity
ADD = mybir.AluOpType.add

FLOPS = 2 * 128 * 1024 * 16384

P = 128
PAIRS = 8
IMG = 35 * 35
PITCH = 1280
ROW = 128


def tile_sparseconv2d_t_kernel(tc, x, weight, bias, out):
    nc = tc.nc
    with ExitStack() as ctx:
        const = ctx.enter_context(tc.tile_pool(name="const", bufs=1))
        spool = ctx.enter_context(tc.tile_pool(name="win", bufs=4))
        qpool = ctx.enter_context(tc.tile_pool(name="codes", bufs=6))
        opool = ctx.enter_context(tc.tile_pool(name="res", bufs=4))
        psum = ctx.enter_context(tc.psum_pool(name="acc", bufs=8))
        ctx.enter_context(tc.manual_schedule())

        xr = x.rearrange("n c h w -> (n c) (h w)").rearrange("(m k r) f -> r k m f", m=PAIRS, k=16, r=8)
        groups = ((0, 1), (1, 2), (2, 4), (4, 8))
        xs = {}
        for m0, m1 in groups:
            xg = const.tile([P, m1 - m0, PITCH], BF16, name="xs%d" % m0)
            for m in range(m0, m1):
                xs[m] = xg[:, m - m0, :]
            xs[(m0, m1)] = xg

        def load_x(queue, r, m0, m1):
            p0 = (r // 2) * 32 + (r % 2)
            queue.dma_start(out=xs[(m0, m1)][p0:p0 + 31:2, :, 0:IMG], in_=xr[r][:, m0:m1, :])

        w_sb = const.tile([P, 1024], BF16)
        nc.sync.dma_start(out=w_sb[:], in_=weight)
        load_x(nc.gpsimd, 7, 0, 1)
        for r in (0, 1, 2, 3):
            load_x(nc.scalar, r, 0, 1)
        for r in (4, 5, 6):
            load_x(nc.sync, r, 0, 1)
        for r in range(8):
            load_x(nc.sync, r, 1, 2)
        b16 = const.tile([P, 1], BF16)
        with nc.allow_non_contiguous_dma(reason="one bias value a partition"):
            nc.sync.dma_start(out=b16[:], in_=bias)
        for m0, m1 in groups[2:]:
            for r in range(8):
                load_x(nc.sync, r, m0, m1)

        wp = const.tile([P, 8 * 144], F32)
        runs = wp[:].rearrange("o (t g k) -> o t g k", t=8, g=9, k=16)
        nc.vector.memset(runs[:, :, 0:9:2, :], 0.0)
        ident = const.tile([P, P], F32)
        make_identity(nc, ident[:])
        warm = const.tile([P, 2], F32)
        nc.vector.memset(warm[:], 0.0)
        nc.scalar.activation(out=warm[:, 1:2], in_=warm[:, 0:1], func=IDENT)

        wins = {}

        def window_tile(m):
            if m not in wins:
                wins[m] = spool.tile([P, 36 * ROW], BF16, align_bytes=64, tag="win", name="win%d" % m)
            return wins[m]

        def copies(m, on_vector, on_scalar):
            win = window_tile(m)
            to = win[:].rearrange("p (h t s e) -> p h t s e", h=18, t=2, s=4, e=32)
            to_words = win[:].bitcast(F32).rearrange("p (h t s e) -> p h t s e", h=18, t=2, s=4, e=16)
            rows_of = xs[m][:, 0:1260].rearrange("p (h e) -> p h e", e=70)
            words_of = xs[m][:, 0:1260].bitcast(F32).rearrange("p (h e) -> p h e", e=35)
            for parity, s in on_vector + on_scalar:
                n = 18 - parity
                start = 35 * parity + s
                if (parity, s) in on_vector:
                    nc.vector.tensor_copy(out=to[:, 0:n, parity, s, :], in_=rows_of[:, 0:n, start:start + 32])
                elif start % 2 == 0:
                    nc.scalar.copy(out=to_words[:, 0:n, parity, s, :], in_=words_of[:, 0:n, start // 2:start // 2 + 16])
                else:
                    nc.scalar.copy(out=to[:, 0:n, parity, s, :], in_=rows_of[:, 0:n, start:start + 32])

        every = tuple((parity, s) for parity in range(2) for s in range(4))
        aligned = tuple(c for c in every if (35 * c[0] + c[1]) % 2 == 0)
        odd = tuple(c for c in every if c not in aligned)

        w_words = w_sb[:].bitcast(F32).rearrange("o (k a e t) -> o t a k e", k=8, a=4, e=2, t=8)

        def sort_weights(i2):
            dst = wp[:].rearrange("o (t g k e) -> o t g k e", t=8, g=9, k=8, e=2)[:, i2 * 4:i2 * 4 + 4, 1:9:2, :, :]
            nc.vector.tensor_copy(out=dst, in_=w_words[:, i2 * 4:i2 * 4 + 4, :, :, :])

        grouped = const.tile([P, 4096], BF16, align_bytes=64)
        gw = grouped[:].bitcast(F32)
        pws = {}

        def transpose_weights(bank):
            i2, nh = bank // 2, bank % 2
            pw = psum.tile([P, 512], F32, tag="acc", name="pw%d" % bank)
            pws[bank] = pw
            for j in range(4):
                first = (i2 * 4 + j) * 144 + 16 * (1 - nh)
                nc.tensor.transpose(pw[:, j * P:(j + 1) * P], wp[:, first:first + P], ident[:])

        def regroup_weights(bank):
            nc.scalar.copy(out=gw[:, bank * 512:(bank + 1) * 512].rearrange("p (s o u) -> p s o u", s=2, o=P, u=2),
                           in_=pws[bank][:].rearrange("p (s u o) -> p s o u", s=2, u=2, o=P))

        wq = const.tile([P, 1024], U32, align_bytes=64)
        wsc = const.tile([P, 1024], U8, align_bytes=64)

        accs = {}

        def quantise(m, i, hf, halves):
            width = 512 * halves
            cd = qpool.tile([P, width], U32, align_bytes=64, tag="cd%d" % halves, name="cd%d_%d_%d" % (m, i, hf))
            sc = qpool.tile([P, width], U8, align_bytes=64, tag="sc%d" % halves, name="sc%d_%d_%d" % (m, i, hf))
            first = (hf * 16 + i) * ROW
            nc.vector.quantize_mx(out=cd[:].bitcast(FP8X4), scales=sc[:], in_=wins[m][:, first:first + 4 * width])
            return cd, sc

        def quarter_step(m, i, qt):
            cd = qpool.tile([P, 256], U32, align_bytes=64, tag="cdq", name="cdq%d_%d_%d" % (m, i, qt))
            sc = qpool.tile([P, 256], U8, align_bytes=64, tag="scq", name="scq%d_%d_%d" % (m, i, qt))
            first = (qt * 8 + i) * ROW
            nc.vector.quantize_mx(out=cd[:].bitcast(FP8X4), scales=sc[:], in_=wins[m][:, first:first + 1024])
            for nh in range(2):
                key = (m, nh, "q%d" % qt)
                if key not in accs:
                    accs[key] = psum.tile([P, 256], F32, tag="acc", name="accq%d_%d_%d" % (m, nh, qt))
                s = (i // 2) * 4 + nh * 2 + i % 2
                nc.tensor.matmul_mx(
                    out=accs[key][:],
                    lhsT=wq[:, s * P:(s + 1) * P].bitcast(FP8X4),
                    lhsT_scale=wsc[:, s * P:(s + 1) * P],
                    rhs=cd[:].bitcast(FP8X4),
                    rhs_scale=sc[:],
                    start=(i == 0),
                    stop=(i == 3),
                )

        def finish_quarter(m, qt, vector_helps):
            for nh in range(2):
                ob = opool.tile([P, 256], F32, tag="obq", name="obq%d_%d_%d" % (m, nh, qt))
                src = accs[(m, nh, "q%d" % qt)][:].rearrange("o (r s q) -> o r q s", r=8, s=4, q=8)
                dst = ob[:].rearrange("o (r q s) -> o r q s", r=8, q=8, s=4)
                if vector_helps and nh == 0:
                    nc.vector.tensor_scalar(out=dst, in0=src, scalar1=b16[:, 0:1], scalar2=None, op0=ADD)
                else:
                    nc.scalar.activation(out=dst, in_=src, func=IDENT, bias=b16[:, 0:1], scale=1.0)
                nc.sync.dma_start(out=out[2 * m + nh].rearrange("o p q -> o (p q)")[:, qt * 256:(qt + 1) * 256],
                                  in_=ob[:])

        def multiply(m, i, hf, halves, cd, sc, images=(0, 1)):
            for h in range(halves):
                for nh in images:
                    key = (m, nh, hf + h)
                    if key not in accs:
                        accs[key] = psum.tile([P, 512], F32, tag="acc", name="acc%d_%d_%d" % key)
                    s = (i // 2) * 4 + nh * 2 + i % 2
                    nc.tensor.matmul_mx(
                        out=accs[key][:],
                        lhsT=wq[:, s * P:(s + 1) * P].bitcast(FP8X4),
                        lhsT_scale=wsc[:, s * P:(s + 1) * P],
                        rhs=cd[:, h * 512:(h + 1) * 512].bitcast(FP8X4),
                        rhs_scale=sc[:, h * 512:(h + 1) * 512],
                        start=(i == 0),
                        stop=(i == 3),
                    )

        def leave(dst, m, nh, hf, on_vector):
            src = accs[(m, nh, hf)][:].rearrange("o (r s q) -> o r q s", r=16, s=4, q=8)
            dst = dst.rearrange("o (r q s) -> o r q s", r=16, q=8, s=4)
            if on_vector:
                nc.vector.tensor_scalar(out=dst, in0=src, scalar1=b16[:, 0:1], scalar2=None, op0=ADD)
            else:
                nc.scalar.activation(out=dst, in_=src, func=IDENT, bias=b16[:, 0:1], scale=1.0)

        def finish(m):
            for nh in range(2):
                ob = opool.tile([P, 1024], F32, tag="ob", name="ob%d_%d" % (m, nh))
                for hf in range(2):
                    leave(ob[:, hf * 512:(hf + 1) * 512], m, nh, hf, False)
                nc.sync.dma_start(out=out[2 * m + nh].rearrange("o p q -> o (p q)"), in_=ob[:])

        def finish_half(m, hf, vector_helps):
            for nh in range(2):
                ob = opool.tile([P, 512], F32, tag="obh", name="obh%d_%d_%d" % (m, nh, hf))
                leave(ob[:], m, nh, hf, vector_helps and nh == 0)
                nc.sync.dma_start(out=out[2 * m + nh].rearrange("o p q -> o (p q)")[:, hf * 512:(hf + 1) * 512],
                                  in_=ob[:])

        def quantise_weights(b0, b1):
            nc.vector.quantize_mx(out=wq[:, b0 * 256:b1 * 256].bitcast(FP8X4), scales=wsc[:, b0 * 256:b1 * 256],
                                  in_=grouped[:, b0 * 1024:b1 * 1024])

        codes = {}
        sort_weights(0)
        sort_weights(1)
        copies(0, odd, ())
        copies(0, (), aligned)
        transpose_weights(0)
        transpose_weights(1)
        transpose_weights(2)
        transpose_weights(3)
        regroup_weights(0)
        regroup_weights(1)
        regroup_weights(2)
        regroup_weights(3)
        copies(1, (), every)
        codes[(0, 0)] = quantise(0, 0, 0, 2)
        quantise_weights(0, 2)
        multiply(0, 0, 0, 2, *codes[(0, 0)])
        codes[(1, 0)] = quantise(0, 1, 0, 2)
        multiply(0, 1, 0, 2, *codes[(1, 0)])
        quantise_weights(2, 4)
        codes[(2, 0)] = quantise(0, 2, 0, 2)
        multiply(0, 2, 0, 2, *codes[(2, 0)])
        codes[(3, 0)] = quantise(0, 3, 0, 2)
        multiply(0, 3, 0, 2, *codes[(3, 0)])
        copies(2, (), every)

        for m in range(1, PAIRS - 1):
            finish(m - 1)
            if m + 2 < PAIRS:
                copies(m + 2, (), every)
            for i in range(4):
                cd, sc = quantise(m, i, 0, 2)
                multiply(m, i, 0, 2, cd, sc)

        m = PAIRS - 1
        finish(m - 1)
        for i in range(4):
            cd, sc = quantise(m, i, 0, 1)
            multiply(m, i, 0, 1, cd, sc)
        finish_half(m, 0, False)
        for qt in (2, 3):
            for i in range(4):
                quarter_step(m, i, qt)
            finish_quarter(m, qt, qt == 3)
